import numpy as np
import ml_dtypes


def mxq(x, axis, fmt="e4m3"):
    dtype, down = {"e4m3": (ml_dtypes.float8_e4m3fn, 7), "e5m2": (ml_dtypes.float8_e5m2, 14)}[fmt]
    v = np.moveaxis(np.asarray(x, np.float32).astype(ml_dtypes.bfloat16).astype(np.float64), axis, -1)
    blocks = v.reshape(v.shape[:-1] + (-1, 32))
    amax = np.abs(blocks).max(-1, keepdims=True)
    byte = np.maximum(np.where(amax > 0, np.frexp(amax)[1] - 1 + 127, 0) - down, 1)
    scale = np.exp2(byte - 127.0)
    codes = (blocks / scale).astype(np.float32).astype(dtype).astype(np.float64)
    return np.moveaxis((codes * scale).reshape(v.shape), -1, axis)


WIDE = False


def mx_kscale(k):
    if not WIDE:
        return np.ones(k)
    levels = np.array([10, -10, 5, -5, 0])
    a = np.random.permutation(np.resize(levels, k // 512 * 4)).reshape(k // 512, 4)
    idx = np.arange(k)
    return np.exp2(a[idx // 512, idx % 128 // 32])


BF16 = ml_dtypes.bfloat16


def bf(x):
    return np.asarray(x, np.float32).astype(BF16)


def f64(x):
    return np.asarray(x).astype(np.float64)


E2M1 = np.array([0.0, 0.5, 1.0, 1.5, 2.0, 3.0, 4.0, 6.0, -0.0, -0.5, -1.0, -1.5, -2.0, -3.0, -4.0, -6.0])


def pack_weight(w, fmt):
    k, n = w.shape
    w = f64(bf(w)).reshape(k // 32, 32, n)
    amax = np.abs(w).max(1)
    if fmt == "e4m3":
        byte = np.frexp(amax)[1] - 1 + 127 - 7
    else:
        mant, ex = np.frexp(amax / 6.0)
        byte = np.where(mant > 0.5, ex, ex - 1) + 127
    byte = np.clip(np.where(amax > 0, byte, 1), 1, 254)
    scaled = (w * np.exp2(127.0 - byte)[:, None, :]).reshape(k, n).astype(np.float32)
    by_word = np.ascontiguousarray(scaled.reshape(k // 512, 128, 4, n).transpose(0, 1, 3, 2))
    if fmt == "e4m3":
        words = by_word.astype(ml_dtypes.float8_e4m3fn).view(np.uint8)
    else:
        c = by_word.astype(ml_dtypes.float4_e2m1fn).view(np.uint8) & 0xF
        words = c[..., 0::2] | (c[..., 1::2] << 4)
    return np.ascontiguousarray(words), np.ascontiguousarray(byte.astype(np.uint8).reshape(k // 512, 16, n))


def unpack_weight(words, scales, fmt):
    g, p, n, _ = words.shape
    if fmt == "e4m3":
        vals = np.ascontiguousarray(words).view(ml_dtypes.float8_e4m3fn).astype(np.float64)
    else:
        nib = np.empty((g, p, n, 4), np.uint8)
        nib[..., 0::2] = words & 0xF
        nib[..., 1::2] = words >> 4
        vals = E2M1[nib]
    vals = vals * np.repeat(np.exp2(scales.astype(np.float64) - 127.0), 8, axis=1)[..., None]
    return vals.transpose(0, 1, 3, 2).reshape(g * 512, n)


B, D_IN, D_OUT = 256, 2048, 2048
FMT = "e4m3"


def sigmoid(v):
    return 1.0 / (1.0 + np.exp(-v))


def setup_inputs():
    s = mx_kscale(D_IN)
    w = lambda: pack_weight(np.random.standard_normal((D_IN, D_OUT)) / np.sqrt(D_IN) / s[:, None], FMT)
    b = lambda: bf(np.random.standard_normal(D_OUT) * 0.5)
    x = bf(np.random.standard_normal((B, D_IN)) * s)
    Wxi_words, Wxi_scales = w()
    bxi = b()
    Wxc_words, Wxc_scales = w()
    bxc = b()
    Wxo_words, Wxo_scales = w()
    bxo = b()
    return {"x": x,
            "Wxi_words": Wxi_words, "Wxi_scales": Wxi_scales, "bxi": bxi,
            "Wxc_words": Wxc_words, "Wxc_scales": Wxc_scales, "bxc": bxc,
            "Wxo_words": Wxo_words, "Wxo_scales": Wxo_scales, "bxo": bxo}


def reference(x, Wxi_words, Wxi_scales, bxi, Wxc_words, Wxc_scales, bxc, Wxo_words, Wxo_scales, bxo):
    xq = mxq(f64(x), 1, "e4m3")
    gi = (xq @ unpack_weight(Wxi_words, Wxi_scales, FMT)) + f64(bxi)
    gc = (xq @ unpack_weight(Wxc_words, Wxc_scales, FMT)) + f64(bxc)
    go = (xq @ unpack_weight(Wxo_words, Wxo_scales, FMT)) + f64(bxo)
    i = sigmoid(gi)
    c = np.tanh(gc)
    o = sigmoid(go)
    new_state = c * i
    return np.tanh(new_state) * o

@@ -1,0 +1,197 @@
+from contextlib import ExitStack
+
+import concourse.mybir as mybir
+from concourse.masks import make_identity
+
+F32 = mybir.dt.float32
+BF16 = mybir.dt.bfloat16
+I32 = mybir.dt.int32
+U32 = mybir.dt.uint32
+U8 = mybir.dt.uint8
+FP8X4 = mybir.dt.float8_e4m3fn_x4
+ADD = mybir.AluOpType.add
+MULT = mybir.AluOpType.mult
+SIGMOID = mybir.ActivationFunctionType.Sigmoid
+TANH = mybir.ActivationFunctionType.Tanh
+
+P = 128
+PACK = 4
+K_PASS = P * PACK
+B, D_IN, D_OUT = 256, 2048, 2048
+GROUPS = D_IN // K_PASS
+ROW_TILES = B // P
+BANK = 512
+SPAN = 1024
+SPANS = D_OUT // SPAN
+BANKS_IN_SPAN = SPAN // BANK
+BLOCKS = D_OUT // BANK
+GATES = 3
+GATE_FUNC = (SIGMOID, TANH, SIGMOID)
+QUADRANTS = 4
+LIVE = 4
+
+FLOPS = 2 * B * D_IN * D_OUT * GATES
+
+
+def tile_lstm_pa_kernel(
+    tc, x, Wxi_words, Wxi_scales, bxi, Wxc_words, Wxc_scales, bxc, Wxo_words, Wxo_scales, bxo, out
+):
+    nc = tc.nc
+    words_in = (Wxi_words, Wxc_words, Wxo_words)
+    scales_in = (Wxi_scales, Wxc_scales, Wxo_scales)
+    bias_in = (bxi, bxc, bxo)
+
+    with ExitStack() as ctx:
+        ctx.enter_context(tc.manual_schedule())
+        keep = ctx.enter_context(tc.tile_pool(name="keep", bufs=1))
+        work = ctx.enter_context(tc.tile_pool(name="work", bufs=6))
+        psum = ctx.enter_context(tc.psum_pool(name="psum", bufs=8))
+
+        ident_bf16 = keep.tile([P, P], BF16)
+        ident_f32 = keep.tile([P, P], F32)
+        table_warmer = keep.tile([P, 1], F32)
+        bias_rows = keep.tile([P, BANK], BF16)
+        bias_all = keep.tile([P, GATES, D_OUT], F32)
+        x_rows = keep.tile([P, ROW_TILES, D_IN], BF16)
+        x_grouped = keep.tile([P, GROUPS, B * PACK], BF16, align_bytes=64)
+        x_codes = keep.tile([P, GROUPS, B], U32, align_bytes=64)
+        x_scales = keep.tile([P, GROUPS, B], U8, align_bytes=64)
+        w_scales = keep.tile([P, GATES, D_OUT], U8, align_bytes=64)
+        w_codes = {}
+        for span in range(SPANS):
+            for gate in range(GATES):
+                for g in range(GROUPS):
+                    w_codes[(span, gate, g)] = keep.tile(
+                        [P, SPAN], U32, name="w_codes_%d_%d_%d" % (span, gate, g), align_bytes=64
+                    )
+
+        nc.vector.memset(bias_rows[:], 0.0)
+        nc.vector.memset(table_warmer[:], 0.0)
+        nc.vector.memset(w_scales[:].bitcast(I32), 0)
+        make_identity(nc, ident_bf16[:])
+        make_identity(nc, ident_f32[:])
+        nc.scalar.activation(out=table_warmer[:], in_=table_warmer[:], func=SIGMOID)
+
+        for gate in range(GATES):
+            nc.sync.dma_start(
+                out=bias_rows[BLOCKS * gate : BLOCKS * (gate + 1), :],
+                in_=bias_in[gate].rearrange("(r c) -> r c", c=BANK),
+            )
+        x_view = x.rearrange("(r p) k -> p r k", p=P)
+        for g in range(GROUPS):
+            k_cols = slice(K_PASS * g, K_PASS * (g + 1))
+            nc.sync.dma_start(out=x_rows[:, :, k_cols], in_=x_view[:, :, k_cols])
+        for gate in range(GATES):
+            for quad in range(QUADRANTS):
+                nc.sync.dma_start(
+                    out=w_scales[32 * quad : 32 * quad + GROUPS * LIVE, gate, :].bitcast(I32),
+                    in_=scales_in[gate][:, LIVE * quad : LIVE * (quad + 1), :].bitcast(I32),
+                )
+        for span in range(SPANS):
+            for gate in range(GATES):
+                for g in range(GROUPS):
+                    source = words_in[gate][g, :, SPAN * span : SPAN * (span + 1), :]
+                    nc.sync.dma_start(
+                        out=w_codes[(span, gate, g)][:].bitcast(I32),
+                        in_=source.rearrange("p n t -> p (n t)").bitcast(I32),
+                    )
+
+        def spread_bias(gate):
+            for block in range(BLOCKS):
+                row = BLOCKS * gate + block
+                spread = psum.tile([P, BANK], F32, tag="bank")
+                nc.tensor.matmul(
+                    out=spread[:],
+                    lhsT=ident_bf16[:, row : row + 1].to_broadcast([P, P]),
+                    rhs=bias_rows[:],
+                    start=True,
+                    stop=True,
+                )
+                target = bias_all[:, gate, BANK * block : BANK * (block + 1)]
+                if block % 2 == 0:
+                    nc.scalar.copy(out=target, in_=spread[:])
+                else:
+                    nc.vector.tensor_copy(out=target, in_=spread[:])
+
+        x_words = x_rows[:].bitcast(F32)
+        words_in_pass = K_PASS // 2
+
+        def turn_group(g):
+            turned = psum.tile([P, 2, B], F32, tag="bank")
+            for r in range(ROW_TILES):
+                for u in range(2):
+                    nc.tensor.transpose(
+                        turned[:, u, P * r : P * (r + 1)],
+                        x_words[:, r, words_in_pass * g + u : words_in_pass * (g + 1) : 2],
+                        ident_f32[:],
+                    )
+            nc.vector.tensor_copy(
+                out=x_grouped[:, g, :].bitcast(F32).rearrange("p (row u) -> p row u", u=2),
+                in_=turned[:].rearrange("p u row -> p row u"),
+            )
+
+        def quantise_group(g):
+            nc.vector.quantize_mx(
+                out=x_codes[:, g, :].bitcast(FP8X4),
+                scales=x_scales[:, g, :],
+                in_=x_grouped[:, g, :],
+            )
+
+        spread_bias(0)
+        for g in range(GROUPS):
+            turn_group(g)
+            if g > 0:
+                quantise_group(g - 1)
+        quantise_group(GROUPS - 1)
+        spread_bias(1)
+        spread_bias(2)
+
+        def product(r, out_ap, in0, in1):
+            engine = nc.gpsimd if r == 0 else nc.vector
+            engine.tensor_tensor(out=out_ap, in0=in0, in1=in1, op=MULT)
+
+        blocks_of_span = [(r, b) for r in range(ROW_TILES) for b in range(BANKS_IN_SPAN)]
+        for span in range(SPANS):
+            value = {}
+            for gate in range(GATES):
+                acc = {}
+                for r, b in blocks_of_span:
+                    acc[(r, b)] = psum.tile([P, BANK], F32, tag="bank", name="acc_%d_%d" % (r, b))
+                for g in range(GROUPS):
+                    for r, b in blocks_of_span:
+                        first = SPAN * span + BANK * b
+                        nc.tensor.matmul_mx(
+                            out=acc[(r, b)][:],
+                            lhsT=x_codes[:, g, P * r : P * (r + 1)].bitcast(FP8X4),
+                            lhsT_scale=x_scales[:, g, P * r : P * (r + 1)],
+                            rhs=w_codes[(span, gate, g)][:, BANK * b : BANK * (b + 1)].bitcast(FP8X4),
+                            rhs_scale=w_scales[LIVE * g : P, gate, first : first + BANK],
+                            start=(g == 0),
+                            stop=(g == GROUPS - 1),
+                        )
+                for r, b in blocks_of_span:
+                    first = SPAN * span + BANK * b
+                    gate_value = work.tile([P, BANK], F32, tag="gate_%d" % gate)
+                    value[(gate, r, b)] = gate_value
+                    nc.vector.tensor_tensor(
+                        out=gate_value[:],
+                        in0=acc[(r, b)][:],
+                        in1=bias_all[:, gate, first : first + BANK],
+                        op=ADD,
+                    )
+                    nc.scalar.activation(out=gate_value[:], in_=gate_value[:], func=GATE_FUNC[gate])
+                if gate == 1:
+                    for r, b in blocks_of_span:
+                        state = value[(1, r, b)]
+                        product(r, state[:], state[:], value[(0, r, b)][:])
+                    for r, b in blocks_of_span:
+                        state = value[(1, r, b)]
+                        nc.scalar.activation(out=state[:], in_=state[:], func=TANH)
+                if gate == 2:
+                    for r, b in blocks_of_span:
+                        first = SPAN * span + BANK * b
+                        result = value[(2, r, b)]
+                        product(r, result[:], result[:], value[(1, r, b)][:])
+                        nc.sync.dma_start(
+                            out=out[P * r : P * (r + 1), first : first + BANK], in_=result[:]
+                        )

@@ -83,9 +83,9 @@ def tile_lstm_pa_kernel(
             nc.sync.dma_start(out=x_rows[:, :, k_cols], in_=x_view[:, :, k_cols])
         for gate in range(GATES):
             for quad in range(QUADRANTS):
-                nc.sync.dma_start(
-                    out=w_scales[32 * quad : 32 * quad + GROUPS * LIVE, gate, :].bitcast(I32),
-                    in_=scales_in[gate][:, LIVE * quad : LIVE * (quad + 1), :].bitcast(I32),
+                nc.gpsimd.dma_start(
+                    out=w_scales[32 * quad : 32 * quad + GROUPS * LIVE, gate, :].bitcast(F32),
+                    in_=scales_in[gate][:, LIVE * quad : LIVE * (quad + 1), :].bitcast(F32),
                 )
         for span in range(SPANS):
             for gate in range(GATES):

@@ -83,9 +83,9 @@ def tile_lstm_pa_kernel(
             nc.sync.dma_start(out=x_rows[:, :, k_cols], in_=x_view[:, :, k_cols])
         for gate in range(GATES):
             for quad in range(QUADRANTS):
-                nc.gpsimd.dma_start(
-                    out=w_scales[32 * quad : 32 * quad + GROUPS * LIVE, gate, :].bitcast(F32),
-                    in_=scales_in[gate][:, LIVE * quad : LIVE * (quad + 1), :].bitcast(F32),
+                nc.sync.dma_start(
+                    out=w_scales[32 * quad : 32 * quad + GROUPS * LIVE, gate, :].bitcast(I32),
+                    in_=scales_in[gate][:, LIVE * quad : LIVE * (quad + 1), :].bitcast(I32),
                 )
         for span in range(SPANS):
             for gate in range(GATES):
@@ -96,22 +96,19 @@ def tile_lstm_pa_kernel(
                         in_=source.rearrange("p n t -> p (n t)").bitcast(I32),
                     )
 
-        def spread_bias(gate):
-            for block in range(BLOCKS):
-                row = BLOCKS * gate + block
-                spread = psum.tile([P, BANK], F32, tag="bank")
-                nc.tensor.matmul(
-                    out=spread[:],
-                    lhsT=ident_bf16[:, row : row + 1].to_broadcast([P, P]),
-                    rhs=bias_rows[:],
-                    start=True,
-                    stop=True,
-                )
-                target = bias_all[:, gate, BANK * block : BANK * (block + 1)]
-                if block % 2 == 0:
-                    nc.scalar.copy(out=target, in_=spread[:])
-                else:
-                    nc.vector.tensor_copy(out=target, in_=spread[:])
+        def spread_bias(row):
+            spread = psum.tile([P, BANK], F32, tag="bank")
+            nc.tensor.matmul(
+                out=spread[:],
+                lhsT=ident_bf16[:, row : row + 1].to_broadcast([P, P]),
+                rhs=bias_rows[:],
+                start=True,
+                stop=True,
+            )
+            nc.scalar.copy(
+                out=bias_all[:].rearrange("p gate n -> p (gate n)")[:, BANK * row : BANK * (row + 1)],
+                in_=spread[:],
+            )
 
         x_words = x_rows[:].bitcast(F32)
         words_in_pass = K_PASS // 2
@@ -119,6 +116,7 @@ def tile_lstm_pa_kernel(
         def turn_group(g):
             turned = psum.tile([P, 2, B], F32, tag="bank")
             for r in range(ROW_TILES):
+                spread_bias(BLOCKS + ROW_TILES * g + r)
                 for u in range(2):
                     nc.tensor.transpose(
                         turned[:, u, P * r : P * (r + 1)],
@@ -137,14 +135,14 @@ def tile_lstm_pa_kernel(
                 in_=x_grouped[:, g, :],
             )
 
-        spread_bias(0)
+        assert (GATES - 1) * BLOCKS == GROUPS * ROW_TILES
+        for row in range(BLOCKS):
+            spread_bias(row)
         for g in range(GROUPS):
             turn_group(g)
             if g > 0:
                 quantise_group(g - 1)
         quantise_group(GROUPS - 1)
-        spread_bias(1)
-        spread_bias(2)
 
         def product(r, out_ap, in0, in1):
             engine = nc.gpsimd if r == 0 else nc.vector

@@ -21,11 +21,12 @@ B, D_IN, D_OUT = 256, 2048, 2048
 GROUPS = D_IN // K_PASS
 ROW_TILES = B // P
 BANK = 512
-SPAN = 1024
+SPAN = 512
 SPANS = D_OUT // SPAN
 BANKS_IN_SPAN = SPAN // BANK
 BLOCKS = D_OUT // BANK
 GATES = 3
+GATE_I, GATE_C, GATE_O = 0, 1, 2
 GATE_FUNC = (SIGMOID, TANH, SIGMOID)
 QUADRANTS = 4
 LIVE = 4
@@ -44,7 +45,7 @@ def tile_lstm_pa_kernel(
     with ExitStack() as ctx:
         ctx.enter_context(tc.manual_schedule())
         keep = ctx.enter_context(tc.tile_pool(name="keep", bufs=1))
-        work = ctx.enter_context(tc.tile_pool(name="work", bufs=6))
+        work = ctx.enter_context(tc.tile_pool(name="work", bufs=8))
         psum = ctx.enter_context(tc.psum_pool(name="psum", bufs=8))
 
         ident_bf16 = keep.tile([P, P], BF16)
@@ -65,6 +66,13 @@ def tile_lstm_pa_kernel(
                         [P, SPAN], U32, name="w_codes_%d_%d_%d" % (span, gate, g), align_bytes=64
                     )
 
+        gate_order = []
+        for span in range(SPANS + 1):
+            if span < SPANS:
+                gate_order.extend([(span, GATE_I), (span, GATE_C)])
+            if span >= 1:
+                gate_order.append((span - 1, GATE_O))
+
         nc.vector.memset(bias_rows[:], 0.0)
         nc.vector.memset(table_warmer[:], 0.0)
         nc.vector.memset(w_scales[:].bitcast(I32), 0)
@@ -83,30 +91,31 @@ def tile_lstm_pa_kernel(
             nc.sync.dma_start(out=x_rows[:, :, k_cols], in_=x_view[:, :, k_cols])
         for gate in range(GATES):
             for quad in range(QUADRANTS):
+                plane_rows = w_scales[32 * quad : 32 * quad + GROUPS * LIVE, gate, :]
+                scale_rows = scales_in[gate][:, LIVE * quad : LIVE * (quad + 1), :]
+                if gate == GATE_I:
+                    nc.sync.dma_start(out=plane_rows.bitcast(I32), in_=scale_rows.bitcast(I32))
+                else:
+                    nc.gpsimd.dma_start(out=plane_rows.bitcast(F32), in_=scale_rows.bitcast(F32))
+        for span, gate in gate_order:
+            for g in range(GROUPS):
+                source = words_in[gate][g, :, SPAN * span : SPAN * (span + 1), :]
                 nc.sync.dma_start(
-                    out=w_scales[32 * quad : 32 * quad + GROUPS * LIVE, gate, :].bitcast(I32),
-                    in_=scales_in[gate][:, LIVE * quad : LIVE * (quad + 1), :].bitcast(I32),
+                    out=w_codes[(span, gate, g)][:].bitcast(I32),
+                    in_=source.rearrange("p n t -> p (n t)").bitcast(I32),
                 )
-        for span in range(SPANS):
-            for gate in range(GATES):
-                for g in range(GROUPS):
-                    source = words_in[gate][g, :, SPAN * span : SPAN * (span + 1), :]
-                    nc.sync.dma_start(
-                        out=w_codes[(span, gate, g)][:].bitcast(I32),
-                        in_=source.rearrange("p n t -> p (n t)").bitcast(I32),
-                    )
 
-        def spread_bias(row):
+        def spread_bias(piece):
             spread = psum.tile([P, BANK], F32, tag="bank")
             nc.tensor.matmul(
                 out=spread[:],
-                lhsT=ident_bf16[:, row : row + 1].to_broadcast([P, P]),
+                lhsT=ident_bf16[:, piece : piece + 1].to_broadcast([P, P]),
                 rhs=bias_rows[:],
                 start=True,
                 stop=True,
             )
             nc.scalar.copy(
-                out=bias_all[:].rearrange("p gate n -> p (gate n)")[:, BANK * row : BANK * (row + 1)],
+                out=bias_all[:].rearrange("p gate n -> p (gate n)")[:, BANK * piece : BANK * (piece + 1)],
                 in_=spread[:],
             )
 
@@ -136,60 +145,74 @@ def tile_lstm_pa_kernel(
             )
 
         assert (GATES - 1) * BLOCKS == GROUPS * ROW_TILES
-        for row in range(BLOCKS):
-            spread_bias(row)
+        for piece in range(BLOCKS):
+            spread_bias(piece)
         for g in range(GROUPS):
             turn_group(g)
             if g > 0:
                 quantise_group(g - 1)
         quantise_group(GROUPS - 1)
 
-        def product(r, out_ap, in0, in1):
-            engine = nc.gpsimd if r == 0 else nc.vector
-            engine.tensor_tensor(out=out_ap, in0=in0, in1=in1, op=MULT)
-
         blocks_of_span = [(r, b) for r in range(ROW_TILES) for b in range(BANKS_IN_SPAN)]
-        for span in range(SPANS):
-            value = {}
-            for gate in range(GATES):
-                acc = {}
-                for r, b in blocks_of_span:
-                    acc[(r, b)] = psum.tile([P, BANK], F32, tag="bank", name="acc_%d_%d" % (r, b))
-                for g in range(GROUPS):
-                    for r, b in blocks_of_span:
-                        first = SPAN * span + BANK * b
-                        nc.tensor.matmul_mx(
-                            out=acc[(r, b)][:],
-                            lhsT=x_codes[:, g, P * r : P * (r + 1)].bitcast(FP8X4),
-                            lhsT_scale=x_scales[:, g, P * r : P * (r + 1)],
-                            rhs=w_codes[(span, gate, g)][:, BANK * b : BANK * (b + 1)].bitcast(FP8X4),
-                            rhs_scale=w_scales[LIVE * g : P, gate, first : first + BANK],
-                            start=(g == 0),
-                            stop=(g == GROUPS - 1),
-                        )
+        value = {}
+
+        def run_gate(span, gate):
+            acc = {}
+            for r, b in blocks_of_span:
+                acc[(r, b)] = psum.tile([P, BANK], F32, tag="bank", name="acc_%d_%d" % (r, b))
+            for g in range(GROUPS):
                 for r, b in blocks_of_span:
                     first = SPAN * span + BANK * b
-                    gate_value = work.tile([P, BANK], F32, tag="gate_%d" % gate)
-                    value[(gate, r, b)] = gate_value
-                    nc.vector.tensor_tensor(
-                        out=gate_value[:],
-                        in0=acc[(r, b)][:],
-                        in1=bias_all[:, gate, first : first + BANK],
-                        op=ADD,
+                    nc.tensor.matmul_mx(
+                        out=acc[(r, b)][:],
+                        lhsT=x_codes[:, g, P * r : P * (r + 1)].bitcast(FP8X4),
+                        lhsT_scale=x_scales[:, g, P * r : P * (r + 1)],
+                        rhs=w_codes[(span, gate, g)][:, BANK * b : BANK * (b + 1)].bitcast(FP8X4),
+                        rhs_scale=w_scales[LIVE * g : P, gate, first : first + BANK],
+                        start=(g == 0),
+                        stop=(g == GROUPS - 1),
                     )
-                    nc.scalar.activation(out=gate_value[:], in_=gate_value[:], func=GATE_FUNC[gate])
-                if gate == 1:
-                    for r, b in blocks_of_span:
-                        state = value[(1, r, b)]
-                        product(r, state[:], state[:], value[(0, r, b)][:])
-                    for r, b in blocks_of_span:
-                        state = value[(1, r, b)]
-                        nc.scalar.activation(out=state[:], in_=state[:], func=TANH)
-                if gate == 2:
-                    for r, b in blocks_of_span:
-                        first = SPAN * span + BANK * b
-                        result = value[(2, r, b)]
-                        product(r, result[:], result[:], value[(1, r, b)][:])
-                        nc.sync.dma_start(
-                            out=out[P * r : P * (r + 1), first : first + BANK], in_=result[:]
-                        )
+            for r, b in blocks_of_span:
+                first = SPAN * span + BANK * b
+                gate_value = work.tile([P, BANK], F32, tag="gate_%d" % gate)
+                value[(span, gate, r, b)] = gate_value
+                nc.vector.tensor_tensor(
+                    out=gate_value[:],
+                    in0=acc[(r, b)][:],
+                    in1=bias_all[:, gate, first : first + BANK],
+                    op=ADD,
+                )
+                nc.scalar.activation(out=gate_value[:], in_=gate_value[:], func=GATE_FUNC[gate])
+
+        def cell_product(span):
+            for r, b in blocks_of_span:
+                state = value[(span, GATE_C, r, b)]
+                nc.gpsimd.tensor_tensor(
+                    out=state[:], in0=state[:], in1=value[(span, GATE_I, r, b)][:], op=MULT
+                )
+
+        def cell_tanh(span):
+            for r, b in blocks_of_span:
+                state = value[(span, GATE_C, r, b)]
+                nc.scalar.activation(out=state[:], in_=state[:], func=TANH)
+
+        def finish(span):
+            for r, b in blocks_of_span:
+                first = SPAN * span + BANK * b
+                result = value[(span, GATE_O, r, b)]
+                nc.vector.tensor_tensor(
+                    out=result[:], in0=result[:], in1=value[(span, GATE_C, r, b)][:], op=MULT
+                )
+                nc.sync.dma_start(out=out[P * r : P * (r + 1), first : first + BANK], in_=result[:])
+
+        for span in range(SPANS + 1):
+            if span < SPANS:
+                run_gate(span, GATE_I)
+                run_gate(span, GATE_C)
+                cell_product(span)
+            if span >= 1:
+                run_gate(span - 1, GATE_O)
+            if span < SPANS:
+                cell_tanh(span)
+            if span >= 1:
+                finish(span - 1)

@@ -66,12 +66,10 @@ def tile_lstm_pa_kernel(
                         [P, SPAN], U32, name="w_codes_%d_%d_%d" % (span, gate, g), align_bytes=64
                     )
 
-        gate_order = []
-        for span in range(SPANS + 1):
-            if span < SPANS:
-                gate_order.extend([(span, GATE_I), (span, GATE_C)])
-            if span >= 1:
-                gate_order.append((span - 1, GATE_O))
+        gate_order = [(0, GATE_I), (1, GATE_I), (0, GATE_C), (1, GATE_C), (2, GATE_I), (0, GATE_O), (2, GATE_C), (1, GATE_O)]
+        for span in range(3, SPANS):
+            gate_order.extend([(span, GATE_I), (span, GATE_C), (span - 1, GATE_O)])
+        gate_order.append((SPANS - 1, GATE_O))
 
         nc.vector.memset(bias_rows[:], 0.0)
         nc.vector.memset(table_warmer[:], 0.0)
@@ -205,14 +203,14 @@ def tile_lstm_pa_kernel(
                 )
                 nc.sync.dma_start(out=out[P * r : P * (r + 1), first : first + BANK], in_=result[:])
 
-        for span in range(SPANS + 1):
-            if span < SPANS:
-                run_gate(span, GATE_I)
-                run_gate(span, GATE_C)
+        waiting = []
+        for span, gate in gate_order:
+            run_gate(span, gate)
+            for due in waiting:
+                cell_tanh(due)
+            waiting.clear()
+            if gate == GATE_C:
                 cell_product(span)
-            if span >= 1:
-                run_gate(span - 1, GATE_O)
-            if span < SPANS:
-                cell_tanh(span)
-            if span >= 1:
-                finish(span - 1)
+                waiting.append(span)
+            if gate == GATE_O:
+                finish(span)

@@ -76,17 +76,15 @@ def tile_lstm_pa_kernel(
         nc.vector.memset(w_scales[:].bitcast(I32), 0)
         make_identity(nc, ident_bf16[:])
         make_identity(nc, ident_f32[:])
-        nc.scalar.activation(out=table_warmer[:], in_=table_warmer[:], func=SIGMOID)
 
         for gate in range(GATES):
-            nc.sync.dma_start(
+            nc.scalar.dma_start(
                 out=bias_rows[BLOCKS * gate : BLOCKS * (gate + 1), :],
                 in_=bias_in[gate].rearrange("(r c) -> r c", c=BANK),
             )
+        nc.scalar.activation(out=table_warmer[:], in_=table_warmer[:], func=SIGMOID)
         x_view = x.rearrange("(r p) k -> p r k", p=P)
-        for g in range(GROUPS):
-            k_cols = slice(K_PASS * g, K_PASS * (g + 1))
-            nc.sync.dma_start(out=x_rows[:, :, k_cols], in_=x_view[:, :, k_cols])
+        nc.sync.dma_start(out=x_rows[:], in_=x_view)
         for gate in range(GATES):
             for quad in range(QUADRANTS):
                 plane_rows = w_scales[32 * quad : 32 * quad + GROUPS * LIVE, gate, :]

@@ -77,29 +77,33 @@ def tile_lstm_pa_kernel(
         make_identity(nc, ident_bf16[:])
         make_identity(nc, ident_f32[:])
 
-        for gate in range(GATES):
-            nc.scalar.dma_start(
-                out=bias_rows[BLOCKS * gate : BLOCKS * (gate + 1), :],
-                in_=bias_in[gate].rearrange("(r c) -> r c", c=BANK),
-            )
         nc.scalar.activation(out=table_warmer[:], in_=table_warmer[:], func=SIGMOID)
         x_view = x.rearrange("(r p) k -> p r k", p=P)
         nc.sync.dma_start(out=x_rows[:], in_=x_view)
+        for gate in range(GATES):
+            nc.sync.dma_start(
+                out=bias_rows[BLOCKS * gate : BLOCKS * (gate + 1), :],
+                in_=bias_in[gate].rearrange("(r c) -> r c", c=BANK),
+            )
+        first_scales = []
         for gate in range(GATES):
             for quad in range(QUADRANTS):
                 plane_rows = w_scales[32 * quad : 32 * quad + GROUPS * LIVE, gate, :]
                 scale_rows = scales_in[gate][:, LIVE * quad : LIVE * (quad + 1), :]
                 if gate == GATE_I:
-                    nc.sync.dma_start(out=plane_rows.bitcast(I32), in_=scale_rows.bitcast(I32))
+                    first_scales.append((plane_rows, scale_rows))
                 else:
                     nc.gpsimd.dma_start(out=plane_rows.bitcast(F32), in_=scale_rows.bitcast(F32))
-        for span, gate in gate_order:
+        for place, (span, gate) in enumerate(gate_order):
             for g in range(GROUPS):
                 source = words_in[gate][g, :, SPAN * span : SPAN * (span + 1), :]
                 nc.sync.dma_start(
                     out=w_codes[(span, gate, g)][:].bitcast(I32),
                     in_=source.rearrange("p n t -> p (n t)").bitcast(I32),
                 )
+            if place == 0:
+                for plane_rows, scale_rows in first_scales:
+                    nc.sync.dma_start(out=plane_rows.bitcast(I32), in_=scale_rows.bitcast(I32))
 
         def spread_bias(piece):
             spread = psum.tile([P, BANK], F32, tag="bank")

@@ -156,6 +156,10 @@ def tile_lstm_pa_kernel(
         blocks_of_span = [(r, b) for r in range(ROW_TILES) for b in range(BANKS_IN_SPAN)]
         value = {}
 
+        def pieces_of(span, gate):
+            width = BANK // 2 if gate == GATE_O and span >= SPANS - 2 else BANK
+            return [slice(first, first + width) for first in range(0, BANK, width)]
+
         def run_gate(span, gate):
             acc = {}
             for r, b in blocks_of_span:
@@ -173,16 +177,20 @@ def tile_lstm_pa_kernel(
                         stop=(g == GROUPS - 1),
                     )
             for r, b in blocks_of_span:
-                first = SPAN * span + BANK * b
                 gate_value = work.tile([P, BANK], F32, tag="gate_%d" % gate)
                 value[(span, gate, r, b)] = gate_value
-                nc.vector.tensor_tensor(
-                    out=gate_value[:],
-                    in0=acc[(r, b)][:],
-                    in1=bias_all[:, gate, first : first + BANK],
-                    op=ADD,
-                )
-                nc.scalar.activation(out=gate_value[:], in_=gate_value[:], func=GATE_FUNC[gate])
+                for piece in pieces_of(span, gate):
+                    first = SPAN * span + BANK * b + piece.start
+                    width = piece.stop - piece.start
+                    nc.vector.tensor_tensor(
+                        out=gate_value[:, piece],
+                        in0=acc[(r, b)][:, piece],
+                        in1=bias_all[:, gate, first : first + width],
+                        op=ADD,
+                    )
+                    nc.scalar.activation(
+                        out=gate_value[:, piece], in_=gate_value[:, piece], func=GATE_FUNC[gate]
+                    )
 
         def cell_product(span):
             for r, b in blocks_of_span:
@@ -198,12 +206,20 @@ def tile_lstm_pa_kernel(
 
         def finish(span):
             for r, b in blocks_of_span:
-                first = SPAN * span + BANK * b
                 result = value[(span, GATE_O, r, b)]
-                nc.vector.tensor_tensor(
-                    out=result[:], in0=result[:], in1=value[(span, GATE_C, r, b)][:], op=MULT
-                )
-                nc.sync.dma_start(out=out[P * r : P * (r + 1), first : first + BANK], in_=result[:])
+                engine = nc.gpsimd if span == SPANS - 2 and r == 1 else nc.vector
+                for piece in pieces_of(span, GATE_O):
+                    first = SPAN * span + BANK * b + piece.start
+                    width = piece.stop - piece.start
+                    engine.tensor_tensor(
+                        out=result[:, piece],
+                        in0=result[:, piece],
+                        in1=value[(span, GATE_C, r, b)][:, piece],
+                        op=MULT,
+                    )
+                    nc.sync.dma_start(
+                        out=out[P * r : P * (r + 1), first : first + width], in_=result[:, piece]
+                    )
 
         waiting = []
         for span, gate in gate_order:

@@ -207,19 +207,15 @@ def tile_lstm_pa_kernel(
         def finish(span):
             for r, b in blocks_of_span:
                 result = value[(span, GATE_O, r, b)]
-                engine = nc.gpsimd if span == SPANS - 2 and r == 1 else nc.vector
                 for piece in pieces_of(span, GATE_O):
-                    first = SPAN * span + BANK * b + piece.start
-                    width = piece.stop - piece.start
-                    engine.tensor_tensor(
+                    nc.vector.tensor_tensor(
                         out=result[:, piece],
                         in0=result[:, piece],
                         in1=value[(span, GATE_C, r, b)][:, piece],
                         op=MULT,
                     )
-                    nc.sync.dma_start(
-                        out=out[P * r : P * (r + 1), first : first + width], in_=result[:, piece]
-                    )
+                first = SPAN * span + BANK * b
+                nc.sync.dma_start(out=out[P * r : P * (r + 1), first : first + BANK], in_=result[:])
 
         waiting = []
         for span, gate in gate_order:

@@ -71,11 +71,12 @@ def tile_lstm_pa_kernel(
             gate_order.extend([(span, GATE_I), (span, GATE_C), (span - 1, GATE_O)])
         gate_order.append((SPANS - 1, GATE_O))
 
+        make_identity(nc, ident_f32[:])
         nc.vector.memset(bias_rows[:], 0.0)
         nc.vector.memset(table_warmer[:], 0.0)
-        nc.vector.memset(w_scales[:].bitcast(I32), 0)
-        make_identity(nc, ident_bf16[:])
-        make_identity(nc, ident_f32[:])
+        for gate in (GATE_C, GATE_O, GATE_I):
+            nc.vector.memset(w_scales[:, gate, :].bitcast(I32), 0)
+        nc.vector.tensor_copy(out=ident_bf16[:], in_=ident_f32[:])
 
         nc.scalar.activation(out=table_warmer[:], in_=table_warmer[:], func=SIGMOID)
         x_view = x.rearrange("(r p) k -> p r k", p=P)
@@ -207,8 +208,9 @@ def tile_lstm_pa_kernel(
         def finish(span):
             for r, b in blocks_of_span:
                 result = value[(span, GATE_O, r, b)]
+                engine = nc.gpsimd if span == SPANS - 2 and r == ROW_TILES - 1 else nc.vector
                 for piece in pieces_of(span, GATE_O):
-                    nc.vector.tensor_tensor(
+                    engine.tensor_tensor(
                         out=result[:, piece],
                         in0=result[:, piece],
                         in1=value[(span, GATE_C, r, b)][:, piece],

from contextlib import ExitStack

import concourse.mybir as mybir
from concourse.masks import make_identity

F32 = mybir.dt.float32
BF16 = mybir.dt.bfloat16
I32 = mybir.dt.int32
U32 = mybir.dt.uint32
U8 = mybir.dt.uint8
FP8X4 = mybir.dt.float8_e4m3fn_x4
ADD = mybir.AluOpType.add
MULT = mybir.AluOpType.mult
SIGMOID = mybir.ActivationFunctionType.Sigmoid
TANH = mybir.ActivationFunctionType.Tanh

P = 128
PACK = 4
K_PASS = P * PACK
B, D_IN, D_OUT = 256, 2048, 2048
GROUPS = D_IN // K_PASS
ROW_TILES = B // P
BANK = 512
SPAN = 512
SPANS = D_OUT // SPAN
BANKS_IN_SPAN = SPAN // BANK
BLOCKS = D_OUT // BANK
GATES = 3
GATE_I, GATE_C, GATE_O = 0, 1, 2
GATE_FUNC = (SIGMOID, TANH, SIGMOID)
QUADRANTS = 4
LIVE = 4

FLOPS = 2 * B * D_IN * D_OUT * GATES


def tile_lstm_pa_kernel(
    tc, x, Wxi_words, Wxi_scales, bxi, Wxc_words, Wxc_scales, bxc, Wxo_words, Wxo_scales, bxo, out
):
    nc = tc.nc
    words_in = (Wxi_words, Wxc_words, Wxo_words)
    scales_in = (Wxi_scales, Wxc_scales, Wxo_scales)
    bias_in = (bxi, bxc, bxo)

    with ExitStack() as ctx:
        ctx.enter_context(tc.manual_schedule())
        keep = ctx.enter_context(tc.tile_pool(name="keep", bufs=1))
        work = ctx.enter_context(tc.tile_pool(name="work", bufs=8))
        psum = ctx.enter_context(tc.psum_pool(name="psum", bufs=8))

        ident_bf16 = keep.tile([P, P], BF16)
        ident_f32 = keep.tile([P, P], F32)
        table_warmer = keep.tile([P, 1], F32)
        bias_rows = keep.tile([P, BANK], BF16)
        bias_all = keep.tile([P, GATES, D_OUT], F32)
        x_rows = keep.tile([P, ROW_TILES, D_IN], BF16)
        x_grouped = keep.tile([P, GROUPS, B * PACK], BF16, align_bytes=64)
        x_codes = keep.tile([P, GROUPS, B], U32, align_bytes=64)
        x_scales = keep.tile([P, GROUPS, B], U8, align_bytes=64)
        w_scales = keep.tile([P, GATES, D_OUT], U8, align_bytes=64)
        w_codes = {}
        for span in range(SPANS):
            for gate in range(GATES):
                for g in range(GROUPS):
                    w_codes[(span, gate, g)] = keep.tile(
                        [P, SPAN], U32, name="w_codes_%d_%d_%d" % (span, gate, g), align_bytes=64
                    )

        gate_order = [(0, GATE_I), (1, GATE_I), (0, GATE_C), (1, GATE_C), (2, GATE_I), (0, GATE_O), (2, GATE_C), (1, GATE_O)]
        for span in range(3, SPANS):
            gate_order.extend([(span, GATE_I), (span, GATE_C), (span - 1, GATE_O)])
        gate_order.append((SPANS - 1, GATE_O))

        make_identity(nc, ident_f32[:])
        nc.vector.memset(bias_rows[:], 0.0)
        nc.vector.memset(table_warmer[:], 0.0)
        for gate in (GATE_C, GATE_O, GATE_I):
            nc.vector.memset(w_scales[:, gate, :].bitcast(I32), 0)
        nc.vector.tensor_copy(out=ident_bf16[:], in_=ident_f32[:])

        nc.scalar.activation(out=table_warmer[:], in_=table_warmer[:], func=SIGMOID)
        x_view = x.rearrange("(r p) k -> p r k", p=P)
        nc.sync.dma_start(out=x_rows[:], in_=x_view)
        for gate in range(GATES):
            nc.sync.dma_start(
                out=bias_rows[BLOCKS * gate : BLOCKS * (gate + 1), :],
                in_=bias_in[gate].rearrange("(r c) -> r c", c=BANK),
            )
        first_scales = []
        for gate in range(GATES):
            for quad in range(QUADRANTS):
                plane_rows = w_scales[32 * quad : 32 * quad + GROUPS * LIVE, gate, :]
                scale_rows = scales_in[gate][:, LIVE * quad : LIVE * (quad + 1), :]
                if gate == GATE_I:
                    first_scales.append((plane_rows, scale_rows))
                else:
                    nc.gpsimd.dma_start(out=plane_rows.bitcast(F32), in_=scale_rows.bitcast(F32))
        for place, (span, gate) in enumerate(gate_order):
            for g in range(GROUPS):
                source = words_in[gate][g, :, SPAN * span : SPAN * (span + 1), :]
                nc.sync.dma_start(
                    out=w_codes[(span, gate, g)][:].bitcast(I32),
                    in_=source.rearrange("p n t -> p (n t)").bitcast(I32),
                )
            if place == 0:
                for plane_rows, scale_rows in first_scales:
                    nc.sync.dma_start(out=plane_rows.bitcast(I32), in_=scale_rows.bitcast(I32))

        def spread_bias(piece):
            spread = psum.tile([P, BANK], F32, tag="bank")
            nc.tensor.matmul(
                out=spread[:],
                lhsT=ident_bf16[:, piece : piece + 1].to_broadcast([P, P]),
                rhs=bias_rows[:],
                start=True,
                stop=True,
            )
            nc.scalar.copy(
                out=bias_all[:].rearrange("p gate n -> p (gate n)")[:, BANK * piece : BANK * (piece + 1)],
                in_=spread[:],
            )

        x_words = x_rows[:].bitcast(F32)
        words_in_pass = K_PASS // 2

        def turn_group(g):
            turned = psum.tile([P, 2, B], F32, tag="bank")
            for r in range(ROW_TILES):
                spread_bias(BLOCKS + ROW_TILES * g + r)
                for u in range(2):
                    nc.tensor.transpose(
                        turned[:, u, P * r : P * (r + 1)],
                        x_words[:, r, words_in_pass * g + u : words_in_pass * (g + 1) : 2],
                        ident_f32[:],
                    )
            nc.vector.tensor_copy(
                out=x_grouped[:, g, :].bitcast(F32).rearrange("p (row u) -> p row u", u=2),
                in_=turned[:].rearrange("p u row -> p row u"),
            )

        def quantise_group(g):
            nc.vector.quantize_mx(
                out=x_codes[:, g, :].bitcast(FP8X4),
                scales=x_scales[:, g, :],
                in_=x_grouped[:, g, :],
            )

        assert (GATES - 1) * BLOCKS == GROUPS * ROW_TILES
        for piece in range(BLOCKS):
            spread_bias(piece)
        for g in range(GROUPS):
            turn_group(g)
            if g > 0:
                quantise_group(g - 1)
        quantise_group(GROUPS - 1)

        blocks_of_span = [(r, b) for r in range(ROW_TILES) for b in range(BANKS_IN_SPAN)]
        value = {}

        def pieces_of(span, gate):
            width = BANK // 2 if gate == GATE_O and span >= SPANS - 2 else BANK
            return [slice(first, first + width) for first in range(0, BANK, width)]

        def run_gate(span, gate):
            acc = {}
            for r, b in blocks_of_span:
                acc[(r, b)] = psum.tile([P, BANK], F32, tag="bank", name="acc_%d_%d" % (r, b))
            for g in range(GROUPS):
                for r, b in blocks_of_span:
                    first = SPAN * span + BANK * b
                    nc.tensor.matmul_mx(
                        out=acc[(r, b)][:],
                        lhsT=x_codes[:, g, P * r : P * (r + 1)].bitcast(FP8X4),
                        lhsT_scale=x_scales[:, g, P * r : P * (r + 1)],
                        rhs=w_codes[(span, gate, g)][:, BANK * b : BANK * (b + 1)].bitcast(FP8X4),
                        rhs_scale=w_scales[LIVE * g : P, gate, first : first + BANK],
                        start=(g == 0),
                        stop=(g == GROUPS - 1),
                    )
            for r, b in blocks_of_span:
                gate_value = work.tile([P, BANK], F32, tag="gate_%d" % gate)
                value[(span, gate, r, b)] = gate_value
                for piece in pieces_of(span, gate):
                    first = SPAN * span + BANK * b + piece.start
                    width = piece.stop - piece.start
                    nc.vector.tensor_tensor(
                        out=gate_value[:, piece],
                        in0=acc[(r, b)][:, piece],
                        in1=bias_all[:, gate, first : first + width],
                        op=ADD,
                    )
                    nc.scalar.activation(
                        out=gate_value[:, piece], in_=gate_value[:, piece], func=GATE_FUNC[gate]
                    )

        def cell_product(span):
            for r, b in blocks_of_span:
                state = value[(span, GATE_C, r, b)]
                nc.gpsimd.tensor_tensor(
                    out=state[:], in0=state[:], in1=value[(span, GATE_I, r, b)][:], op=MULT
                )

        def cell_tanh(span):
            for r, b in blocks_of_span:
                state = value[(span, GATE_C, r, b)]
                nc.scalar.activation(out=state[:], in_=state[:], func=TANH)

        def finish(span):
            for r, b in blocks_of_span:
                result = value[(span, GATE_O, r, b)]
                engine = nc.gpsimd if span == SPANS - 2 and r == ROW_TILES - 1 else nc.vector
                for piece in pieces_of(span, GATE_O):
                    engine.tensor_tensor(
                        out=result[:, piece],
                        in0=result[:, piece],
                        in1=value[(span, GATE_C, r, b)][:, piece],
                        op=MULT,
                    )
                first = SPAN * span + BANK * b
                nc.sync.dma_start(out=out[P * r : P * (r + 1), first : first + BANK], in_=result[:])

        waiting = []
        for span, gate in gate_order:
            run_gate(span, gate)
            for due in waiting:
                cell_tanh(due)
            waiting.clear()
            if gate == GATE_C:
                cell_product(span)
                waiting.append(span)
            if gate == GATE_O:
                finish(span)
